import numpy as np
import ml_dtypes

BF16 = ml_dtypes.bfloat16


def bf(x):
    return np.asarray(x, np.float32).astype(BF16)


def f32(x):
    return np.asarray(x, np.float32)


def f64(x):
    return np.asarray(x).astype(np.float64)


def striped(idx):
    return np.tile(idx.reshape(-1, 16).T, (8, 1))


C, S, N = 768, 2048, 512
EPS = 1e-5


def setup_inputs():
    return {
        "wte": f32(np.random.standard_normal((C, S))),
        "wpe": f32(0.5 * np.random.standard_normal((C, N))),
        "gain": f32(1.0 + 0.1 * np.random.standard_normal((C, 1))),
        "bias": f32(0.1 * np.random.standard_normal((C, 1))),
        "offs": striped(np.random.permutation(np.tile(np.arange(S), 2))[:N]),
    }


def reference(wte, wpe, gain, bias, offs):
    idx = offs[:16].T.reshape(-1)
    x = f64(wte)[:, idx] + f64(wpe)
    mu = x.mean(axis=0, keepdims=True)
    var = ((x - mu) ** 2).mean(axis=0, keepdims=True)
    y = (x - mu) / np.sqrt(var + EPS) * f64(gain) + f64(bias)
    return np.concatenate([x, y], axis=1)

@@ -1,0 +1,84 @@
+import concourse.masks as masks
+import concourse.mybir as mybir
+
+F32 = mybir.dt.float32
+U16 = mybir.dt.uint16
+ALU = mybir.AluOpType
+ACT = mybir.ActivationFunctionType
+
+P = 128
+C, S, N = 768, 2048, 512
+NB = C // P
+EPS = 1e-5
+
+
+def tile_trunk_model_kernel(tc, wte, wpe, gain, bias, offs, out):
+    nc = tc.nc
+    with (
+        tc.tile_pool(name="held", bufs=1) as held,
+        tc.tile_pool(name="work", bufs=2) as work,
+        tc.psum_pool(name="psum", bufs=1) as psum,
+    ):
+        offsets = held.tile([P, N // 16], U16, name="offsets")
+        nc.sync.dma_start(offsets[:], offs)
+        table = [held.tile([P, S], F32, name=f"table{b}") for b in range(NB)]
+        pos = [held.tile([P, N], F32, name=f"pos{b}") for b in range(NB)]
+        for b in range(NB):
+            rows = slice(b * P, (b + 1) * P)
+            nc.sync.dma_start(pos[b][:], wpe[rows, :])
+            nc.sync.dma_start(table[b][:], wte[rows, :])
+
+        rows_gb = held.tile([P, P], F32, name="rows_gb")
+        nc.vector.memset(rows_gb[:], 0.0)
+        nc.scalar.dma_start(rows_gb[0:NB, :], gain.rearrange("(b p) o -> b (p o)", p=P))
+        nc.scalar.dma_start(rows_gb[NB : 2 * NB, :], bias.rearrange("(b p) o -> b (p o)", p=P))
+        identity = held.tile([P, P], F32, name="identity")
+        masks.make_identity(nc, identity[:])
+        turned_gb = psum.tile([P, P], F32, name="turned_gb")
+        nc.tensor.transpose(turned_gb[:], rows_gb[:], identity[:])
+        gain_bias = held.tile([P, 2 * NB], F32, name="gain_bias")
+        nc.vector.tensor_copy(gain_bias[:], turned_gb[:, 0 : 2 * NB])
+
+        mean_of_block = held.tile([P, P], F32, name="mean_of_block")
+        nc.vector.memset(mean_of_block[:], 1.0 / P)
+        mean_of_all = held.tile([P, P], F32, name="mean_of_all")
+        nc.vector.memset(mean_of_all[:], 1.0 / C)
+        eps = held.tile([P, 1], F32, name="eps")
+        nc.vector.memset(eps[:], EPS)
+        warm = held.tile([P, 1], F32, name="warm")
+        nc.scalar.activation(warm[:], eps[:], ACT.Abs_reciprocal_sqrt)
+
+        shift = psum.tile([P, N], F32, name="shift")
+        mean_d = psum.tile([P, N], F32, name="mean_d")
+        mean_d2 = psum.tile([P, N], F32, name="mean_d2")
+        x = [held.tile([P, N], F32, name=f"x{b}") for b in range(NB)]
+        d = [held.tile([P, N], F32, name=f"d{b}") for b in range(NB)]
+        for b in range(NB):
+            nc.vector.tensor_tensor(x[b][:], table[b][:].indirect(offsets[:]), pos[b][:], ALU.add)
+            nc.sync.dma_start(out[b * P : (b + 1) * P, 0:N], x[b][:])
+            if b == 0:
+                nc.tensor.matmul(shift[:], mean_of_block[:], x[0][:], start=True, stop=True)
+            nc.vector.tensor_tensor(d[b][:], x[b][:], shift[:], ALU.subtract)
+            d2 = work.tile([P, N], F32, name="d2")
+            nc.scalar.activation(d2[:], d[b][:], ACT.Square)
+            nc.tensor.matmul(mean_d[:], mean_of_all[:], d[b][:], start=(b == 0), stop=(b == NB - 1))
+            nc.tensor.matmul(mean_d2[:], mean_of_all[:], d2[:], start=(b == 0), stop=(b == NB - 1))
+
+        square_of_mean = held.tile([P, N], F32, name="square_of_mean")
+        nc.scalar.activation(square_of_mean[:], mean_d[:], ACT.Square)
+        var = held.tile([P, N], F32, name="var")
+        nc.vector.tensor_tensor(var[:], mean_d2[:], square_of_mean[:], ALU.subtract)
+        rstd = held.tile([P, N], F32, name="rstd")
+        nc.scalar.activation(rstd[:], var[:], ACT.Abs_reciprocal_sqrt, bias=eps[:])
+
+        for b in range(NB):
+            centred = work.tile([P, N], F32, name="centred")
+            nc.vector.tensor_tensor(centred[:], d[b][:], mean_d[:], ALU.subtract)
+            normed = work.tile([P, N], F32, name="normed")
+            nc.vector.tensor_tensor(normed[:], centred[:], rstd[:], ALU.mult)
+            y = work.tile([P, N], F32, name="y")
+            nc.scalar.activation(
+                y[:], normed[:], ACT.Identity,
+                bias=gain_bias[:, NB + b : NB + b + 1], scale=gain_bias[:, b : b + 1],
+            )
+            nc.sync.dma_start(out[b * P : (b + 1) * P, N : 2 * N], y[:])

@@ -9,6 +9,8 @@ ACT = mybir.ActivationFunctionType
 P = 128
 C, S, N = 768, 2048, 512
 NB = C // P
+H = 2
+NH = N // H
 EPS = 1e-5
 
 
@@ -16,7 +18,8 @@ def tile_trunk_model_kernel(tc, wte, wpe, gain, bias, offs, out):
     nc = tc.nc
     with (
         tc.tile_pool(name="held", bufs=1) as held,
-        tc.tile_pool(name="work", bufs=2) as work,
+        tc.tile_pool(name="work", bufs=4) as work,
+        tc.tile_pool(name="tail", bufs=NB * H) as tail,
         tc.psum_pool(name="psum", bufs=1) as psum,
     ):
         offsets = held.tile([P, N // 16], U16, name="offsets")
@@ -49,36 +52,47 @@ def tile_trunk_model_kernel(tc, wte, wpe, gain, bias, offs, out):
         nc.scalar.activation(warm[:], eps[:], ACT.Abs_reciprocal_sqrt)
 
         shift = psum.tile([P, N], F32, name="shift")
-        mean_d = psum.tile([P, N], F32, name="mean_d")
-        mean_d2 = psum.tile([P, N], F32, name="mean_d2")
+        sum_d = [psum.tile([P, NH], F32, name=f"sum_d{h}") for h in range(H)]
+        sum_d2 = [psum.tile([P, NH], F32, name=f"sum_d2{h}") for h in range(H)]
         x = [held.tile([P, N], F32, name=f"x{b}") for b in range(NB)]
         d = [held.tile([P, N], F32, name=f"d{b}") for b in range(NB)]
         for b in range(NB):
-            nc.vector.tensor_tensor(x[b][:], table[b][:].indirect(offsets[:]), pos[b][:], ALU.add)
+            first, last = b == 0, b == NB - 1
+            for h in range(H):
+                cols = slice(h * NH, (h + 1) * NH)
+                picked = table[b][:].indirect(offsets[:, h * (NH // 16) : (h + 1) * (NH // 16)])
+                nc.vector.tensor_tensor(x[b][:, cols], picked, pos[b][:, cols], ALU.add)
+                if first:
+                    nc.tensor.matmul(shift[:, cols], mean_of_block[:], x[0][:, cols], start=True, stop=True)
+                nc.vector.tensor_tensor(d[b][:, cols], x[b][:, cols], shift[:, cols], ALU.subtract)
+                d2 = work.tile([P, NH], F32, name="d2")
+                nc.scalar.activation(d2[:], d[b][:, cols], ACT.Square)
+                nc.tensor.matmul(sum_d[h][:], mean_of_all[:], d[b][:, cols], start=first, stop=last)
+                nc.tensor.matmul(sum_d2[h][:], mean_of_all[:], d2[:], start=first, stop=last)
             nc.sync.dma_start(out[b * P : (b + 1) * P, 0:N], x[b][:])
-            if b == 0:
-                nc.tensor.matmul(shift[:], mean_of_block[:], x[0][:], start=True, stop=True)
-            nc.vector.tensor_tensor(d[b][:], x[b][:], shift[:], ALU.subtract)
-            d2 = work.tile([P, N], F32, name="d2")
-            nc.scalar.activation(d2[:], d[b][:], ACT.Square)
-            nc.tensor.matmul(mean_d[:], mean_of_all[:], d[b][:], start=(b == 0), stop=(b == NB - 1))
-            nc.tensor.matmul(mean_d2[:], mean_of_all[:], d2[:], start=(b == 0), stop=(b == NB - 1))
 
-        square_of_mean = held.tile([P, N], F32, name="square_of_mean")
-        nc.scalar.activation(square_of_mean[:], mean_d[:], ACT.Square)
-        var = held.tile([P, N], F32, name="var")
-        nc.vector.tensor_tensor(var[:], mean_d2[:], square_of_mean[:], ALU.subtract)
+        mean_d = held.tile([P, N], F32, name="mean_d")
         rstd = held.tile([P, N], F32, name="rstd")
-        nc.scalar.activation(rstd[:], var[:], ACT.Abs_reciprocal_sqrt, bias=eps[:])
+        for h in range(H):
+            cols = slice(h * NH, (h + 1) * NH)
+            nc.scalar.copy(mean_d[:, cols], sum_d[h][:])
+            square_of_mean = work.tile([P, NH], F32, name="square_of_mean")
+            nc.scalar.activation(square_of_mean[:], sum_d[h][:], ACT.Square)
+            var = work.tile([P, NH], F32, name="var")
+            nc.vector.tensor_tensor(var[:], sum_d2[h][:], square_of_mean[:], ALU.subtract)
+            nc.scalar.activation(rstd[:, cols], var[:], ACT.Abs_reciprocal_sqrt, bias=eps[:])
 
-        for b in range(NB):
-            centred = work.tile([P, N], F32, name="centred")
-            nc.vector.tensor_tensor(centred[:], d[b][:], mean_d[:], ALU.subtract)
-            normed = work.tile([P, N], F32, name="normed")
-            nc.vector.tensor_tensor(normed[:], centred[:], rstd[:], ALU.mult)
-            y = work.tile([P, N], F32, name="y")
-            nc.scalar.activation(
-                y[:], normed[:], ACT.Identity,
-                bias=gain_bias[:, NB + b : NB + b + 1], scale=gain_bias[:, b : b + 1],
-            )
-            nc.sync.dma_start(out[b * P : (b + 1) * P, N : 2 * N], y[:])
+        for h in range(H):
+            cols = slice(h * NH, (h + 1) * NH)
+            for b in range(NB):
+                engine = nc.gpsimd if b % 3 == 2 else nc.vector
+                centred = tail.tile([P, NH], F32, name="centred")
+                engine.tensor_tensor(centred[:], d[b][:, cols], mean_d[:, cols], ALU.subtract)
+                normed = tail.tile([P, NH], F32, name="normed")
+                engine.tensor_tensor(normed[:], centred[:], rstd[:, cols], ALU.mult)
+                y = tail.tile([P, NH], F32, name="y")
+                nc.scalar.activation(
+                    y[:], normed[:], ACT.Identity,
+                    bias=gain_bias[:, NB + b : NB + b + 1], scale=gain_bias[:, b : b + 1],
+                )
+                nc.sync.dma_start(out[b * P : (b + 1) * P, N + h * NH : N + (h + 1) * NH], y[:])

@@ -85,11 +85,10 @@ def tile_trunk_model_kernel(tc, wte, wpe, gain, bias, offs, out):
         for h in range(H):
             cols = slice(h * NH, (h + 1) * NH)
             for b in range(NB):
-                engine = nc.gpsimd if b % 3 == 2 else nc.vector
                 centred = tail.tile([P, NH], F32, name="centred")
-                engine.tensor_tensor(centred[:], d[b][:, cols], mean_d[:, cols], ALU.subtract)
+                nc.vector.tensor_tensor(centred[:], d[b][:, cols], mean_d[:, cols], ALU.subtract)
                 normed = tail.tile([P, NH], F32, name="normed")
-                engine.tensor_tensor(normed[:], centred[:], rstd[:, cols], ALU.mult)
+                nc.vector.tensor_tensor(normed[:], centred[:], rstd[:, cols], ALU.mult)
                 y = tail.tile([P, NH], F32, name="y")
                 nc.scalar.activation(
                     y[:], normed[:], ACT.Identity,

@@ -55,7 +55,7 @@ def tile_trunk_model_kernel(tc, wte, wpe, gain, bias, offs, out):
         sum_d = [psum.tile([P, NH], F32, name=f"sum_d{h}") for h in range(H)]
         sum_d2 = [psum.tile([P, NH], F32, name=f"sum_d2{h}") for h in range(H)]
         x = [held.tile([P, N], F32, name=f"x{b}") for b in range(NB)]
-        d = [held.tile([P, N], F32, name=f"d{b}") for b in range(NB)]
+        d = held.tile([P, NB, N], F32, name="d")
         for b in range(NB):
             first, last = b == 0, b == NB - 1
             for h in range(H):
@@ -64,16 +64,18 @@ def tile_trunk_model_kernel(tc, wte, wpe, gain, bias, offs, out):
                 nc.vector.tensor_tensor(x[b][:, cols], picked, pos[b][:, cols], ALU.add)
                 if first:
                     nc.tensor.matmul(shift[:, cols], mean_of_block[:], x[0][:, cols], start=True, stop=True)
-                nc.vector.tensor_tensor(d[b][:, cols], x[b][:, cols], shift[:, cols], ALU.subtract)
+                nc.vector.tensor_tensor(d[:, b, cols], x[b][:, cols], shift[:, cols], ALU.subtract)
                 d2 = work.tile([P, NH], F32, name="d2")
-                nc.scalar.activation(d2[:], d[b][:, cols], ACT.Square)
-                nc.tensor.matmul(sum_d[h][:], mean_of_all[:], d[b][:, cols], start=first, stop=last)
+                nc.scalar.activation(d2[:], d[:, b, cols], ACT.Square)
+                nc.tensor.matmul(sum_d[h][:], mean_of_all[:], d[:, b, cols], start=first, stop=last)
                 nc.tensor.matmul(sum_d2[h][:], mean_of_all[:], d2[:], start=first, stop=last)
             nc.sync.dma_start(out[b * P : (b + 1) * P, 0:N], x[b][:])
 
         mean_d = held.tile([P, N], F32, name="mean_d")
         rstd = held.tile([P, N], F32, name="rstd")
-        for h in range(H):
+        centred = held.tile([P, NB, N], F32, name="centred")
+
+        def statistics(h):
             cols = slice(h * NH, (h + 1) * NH)
             nc.scalar.copy(mean_d[:, cols], sum_d[h][:])
             square_of_mean = work.tile([P, NH], F32, name="square_of_mean")
@@ -82,16 +84,26 @@ def tile_trunk_model_kernel(tc, wte, wpe, gain, bias, offs, out):
             nc.vector.tensor_tensor(var[:], sum_d2[h][:], square_of_mean[:], ALU.subtract)
             nc.scalar.activation(rstd[:, cols], var[:], ACT.Abs_reciprocal_sqrt, bias=eps[:])
 
-        for h in range(H):
+        def centre(h):
+            cols = slice(h * NH, (h + 1) * NH)
+            repeated = mean_d[:, cols].unsqueeze(1).to_broadcast([P, NB, NH])
+            nc.vector.tensor_tensor(centred[:, :, cols], d[:, :, cols], repeated, ALU.subtract)
+
+        def finish(h):
             cols = slice(h * NH, (h + 1) * NH)
             for b in range(NB):
-                centred = tail.tile([P, NH], F32, name="centred")
-                nc.vector.tensor_tensor(centred[:], d[b][:, cols], mean_d[:, cols], ALU.subtract)
                 normed = tail.tile([P, NH], F32, name="normed")
-                nc.vector.tensor_tensor(normed[:], centred[:], rstd[:, cols], ALU.mult)
+                nc.vector.tensor_tensor(normed[:], centred[:, b, cols], rstd[:, cols], ALU.mult)
                 y = tail.tile([P, NH], F32, name="y")
                 nc.scalar.activation(
                     y[:], normed[:], ACT.Identity,
                     bias=gain_bias[:, NB + b : NB + b + 1], scale=gain_bias[:, b : b + 1],
                 )
                 nc.sync.dma_start(out[b * P : (b + 1) * P, N + h * NH : N + (h + 1) * NH], y[:])
+
+        statistics(0)
+        centre(0)
+        statistics(1)
+        finish(0)
+        centre(1)
+        finish(1)

@@ -10,6 +10,7 @@ P = 128
 C, S, N = 768, 2048, 512
 NB = C // P
 H = 2
+NV = 4
 NH = N // H
 EPS = 1e-5
 
@@ -73,6 +74,7 @@ def tile_trunk_model_kernel(tc, wte, wpe, gain, bias, offs, out):
 
         mean_d = held.tile([P, N], F32, name="mean_d")
         rstd = held.tile([P, N], F32, name="rstd")
+        rstd_psum = [psum.tile([P, NH], F32, name=f"rstd_psum{h}") for h in range(H)]
         centred = held.tile([P, NB, N], F32, name="centred")
 
         def statistics(h):
@@ -83,17 +85,27 @@ def tile_trunk_model_kernel(tc, wte, wpe, gain, bias, offs, out):
             var = work.tile([P, NH], F32, name="var")
             nc.vector.tensor_tensor(var[:], sum_d2[h][:], square_of_mean[:], ALU.subtract)
             nc.scalar.activation(rstd[:, cols], var[:], ACT.Abs_reciprocal_sqrt, bias=eps[:])
+            nc.tensor.matmul(rstd_psum[h][:], identity[:], rstd[:, cols], start=True, stop=True)
 
         def centre(h):
             cols = slice(h * NH, (h + 1) * NH)
-            repeated = mean_d[:, cols].unsqueeze(1).to_broadcast([P, NB, NH])
-            nc.vector.tensor_tensor(centred[:, :, cols], d[:, :, cols], repeated, ALU.subtract)
+            nc.vector.tensor_tensor(
+                centred[:, 0:NV, cols], d[:, 0:NV, cols],
+                sum_d[h][:].unsqueeze(1).to_broadcast([P, NV, NH]), ALU.subtract,
+            )
+            nc.gpsimd.tensor_tensor(
+                centred[:, NV:NB, cols], d[:, NV:NB, cols],
+                mean_d[:, cols].unsqueeze(1).to_broadcast([P, NB - NV, NH]), ALU.subtract,
+            )
 
         def finish(h):
             cols = slice(h * NH, (h + 1) * NH)
             for b in range(NB):
                 normed = tail.tile([P, NH], F32, name="normed")
-                nc.vector.tensor_tensor(normed[:], centred[:, b, cols], rstd[:, cols], ALU.mult)
+                if b < NV:
+                    nc.vector.tensor_tensor(normed[:], centred[:, b, cols], rstd_psum[h][:], ALU.mult)
+                else:
+                    nc.gpsimd.tensor_tensor(normed[:], centred[:, b, cols], rstd[:, cols], ALU.mult)
                 y = tail.tile([P, NH], F32, name="y")
                 nc.scalar.activation(
                     y[:], normed[:], ACT.Identity,

@@ -100,17 +100,19 @@ def tile_trunk_model_kernel(tc, wte, wpe, gain, bias, offs, out):
 
         def finish(h):
             cols = slice(h * NH, (h + 1) * NH)
+            normed = [tail.tile([P, NH], F32, name="normed") for b in range(NB)]
             for b in range(NB):
-                normed = tail.tile([P, NH], F32, name="normed")
                 if b < NV:
-                    nc.vector.tensor_tensor(normed[:], centred[:, b, cols], rstd_psum[h][:], ALU.mult)
+                    nc.vector.tensor_tensor(normed[b][:], centred[:, b, cols], rstd_psum[h][:], ALU.mult)
                 else:
-                    nc.gpsimd.tensor_tensor(normed[:], centred[:, b, cols], rstd[:, cols], ALU.mult)
+                    nc.gpsimd.tensor_tensor(normed[b][:], centred[:, b, cols], rstd[:, cols], ALU.mult)
+            for b in range(NB):
+                gain_b, bias_b = gain_bias[:, b : b + 1], gain_bias[:, NB + b : NB + b + 1]
                 y = tail.tile([P, NH], F32, name="y")
-                nc.scalar.activation(
-                    y[:], normed[:], ACT.Identity,
-                    bias=gain_bias[:, NB + b : NB + b + 1], scale=gain_bias[:, b : b + 1],
-                )
+                if h == H - 1 and b < NV:
+                    nc.vector.tensor_scalar(y[:], normed[b][:], gain_b, bias_b, ALU.mult, ALU.add)
+                else:
+                    nc.scalar.activation(y[:], normed[b][:], ACT.Identity, bias=bias_b, scale=gain_b)
                 nc.sync.dma_start(out[b * P : (b + 1) * P, N + h * NH : N + (h + 1) * NH], y[:])
 
         statistics(0)

@@ -79,20 +79,18 @@ def tile_trunk_model_kernel(tc, wte, wpe, gain, bias, offs, out):
 
         def statistics(h):
             cols = slice(h * NH, (h + 1) * NH)
-            nc.scalar.copy(mean_d[:, cols], sum_d[h][:])
             square_of_mean = work.tile([P, NH], F32, name="square_of_mean")
             nc.scalar.activation(square_of_mean[:], sum_d[h][:], ACT.Square)
             var = work.tile([P, NH], F32, name="var")
             nc.vector.tensor_tensor(var[:], sum_d2[h][:], square_of_mean[:], ALU.subtract)
             nc.scalar.activation(rstd[:, cols], var[:], ACT.Abs_reciprocal_sqrt, bias=eps[:])
             nc.tensor.matmul(rstd_psum[h][:], identity[:], rstd[:, cols], start=True, stop=True)
+            nc.scalar.copy(mean_d[:, cols], sum_d[h][:])
 
         def centre(h):
             cols = slice(h * NH, (h + 1) * NH)
-            nc.vector.tensor_tensor(
-                centred[:, 0:NV, cols], d[:, 0:NV, cols],
-                sum_d[h][:].unsqueeze(1).to_broadcast([P, NV, NH]), ALU.subtract,
-            )
+            for b in range(NV):
+                nc.vector.tensor_tensor(centred[:, b, cols], d[:, b, cols], sum_d[h][:], ALU.subtract)
             nc.gpsimd.tensor_tensor(
                 centred[:, NV:NB, cols], d[:, NV:NB, cols],
                 mean_d[:, cols].unsqueeze(1).to_broadcast([P, NB - NV, NH]), ALU.subtract,
@@ -100,19 +98,17 @@ def tile_trunk_model_kernel(tc, wte, wpe, gain, bias, offs, out):
 
         def finish(h):
             cols = slice(h * NH, (h + 1) * NH)
-            normed = [tail.tile([P, NH], F32, name="normed") for b in range(NB)]
             for b in range(NB):
+                normed = tail.tile([P, NH], F32, name="normed")
                 if b < NV:
-                    nc.vector.tensor_tensor(normed[b][:], centred[:, b, cols], rstd_psum[h][:], ALU.mult)
+                    nc.vector.tensor_tensor(normed[:], centred[:, b, cols], rstd_psum[h][:], ALU.mult)
                 else:
-                    nc.gpsimd.tensor_tensor(normed[b][:], centred[:, b, cols], rstd[:, cols], ALU.mult)
-            for b in range(NB):
-                gain_b, bias_b = gain_bias[:, b : b + 1], gain_bias[:, NB + b : NB + b + 1]
+                    nc.gpsimd.tensor_tensor(normed[:], centred[:, b, cols], rstd[:, cols], ALU.mult)
                 y = tail.tile([P, NH], F32, name="y")
-                if h == H - 1 and b < NV:
-                    nc.vector.tensor_scalar(y[:], normed[b][:], gain_b, bias_b, ALU.mult, ALU.add)
-                else:
-                    nc.scalar.activation(y[:], normed[b][:], ACT.Identity, bias=bias_b, scale=gain_b)
+                nc.scalar.activation(
+                    y[:], normed[:], ACT.Identity,
+                    bias=gain_bias[:, NB + b : NB + b + 1], scale=gain_bias[:, b : b + 1],
+                )
                 nc.sync.dma_start(out[b * P : (b + 1) * P, N + h * NH : N + (h + 1) * NH], y[:])
 
         statistics(0)

@@ -9,9 +9,8 @@ ACT = mybir.ActivationFunctionType
 P = 128
 C, S, N = 768, 2048, 512
 NB = C // P
-H = 2
-NV = 4
-NH = N // H
+NT = N // P
+STATS = 6
 EPS = 1e-5
 
 
@@ -19,9 +18,7 @@ def tile_trunk_model_kernel(tc, wte, wpe, gain, bias, offs, out):
     nc = tc.nc
     with (
         tc.tile_pool(name="held", bufs=1) as held,
-        tc.tile_pool(name="work", bufs=4) as work,
-        tc.tile_pool(name="tail", bufs=NB * H) as tail,
-        tc.psum_pool(name="psum", bufs=1) as psum,
+        tc.psum_pool(name="psum", bufs=8) as psum,
     ):
         offsets = held.tile([P, N // 16], U16, name="offsets")
         nc.sync.dma_start(offsets[:], offs)
@@ -38,82 +35,55 @@ def tile_trunk_model_kernel(tc, wte, wpe, gain, bias, offs, out):
         nc.scalar.dma_start(rows_gb[NB : 2 * NB, :], bias.rearrange("(b p) o -> b (p o)", p=P))
         identity = held.tile([P, P], F32, name="identity")
         masks.make_identity(nc, identity[:])
-        turned_gb = psum.tile([P, P], F32, name="turned_gb")
+        turned_gb = psum.tile([P, P], F32, name="turned_gb", tag="turned")
         nc.tensor.transpose(turned_gb[:], rows_gb[:], identity[:])
         gain_bias = held.tile([P, 2 * NB], F32, name="gain_bias")
         nc.vector.tensor_copy(gain_bias[:], turned_gb[:, 0 : 2 * NB])
 
-        mean_of_block = held.tile([P, P], F32, name="mean_of_block")
-        nc.vector.memset(mean_of_block[:], 1.0 / P)
-        mean_of_all = held.tile([P, P], F32, name="mean_of_all")
-        nc.vector.memset(mean_of_all[:], 1.0 / C)
         eps = held.tile([P, 1], F32, name="eps")
         nc.vector.memset(eps[:], EPS)
         warm = held.tile([P, 1], F32, name="warm")
         nc.scalar.activation(warm[:], eps[:], ACT.Abs_reciprocal_sqrt)
 
-        shift = psum.tile([P, N], F32, name="shift")
-        sum_d = [psum.tile([P, NH], F32, name=f"sum_d{h}") for h in range(H)]
-        sum_d2 = [psum.tile([P, NH], F32, name=f"sum_d2{h}") for h in range(H)]
-        x = [held.tile([P, N], F32, name=f"x{b}") for b in range(NB)]
-        d = held.tile([P, NB, N], F32, name="d")
+        x = held.tile([P, NB, N], F32, name="x")
+        x_turned = held.tile([P, NT, C], F32, name="x_turned")
+        stats = held.tile([P, NT, NB, STATS], F32, name="stats")
         for b in range(NB):
-            first, last = b == 0, b == NB - 1
-            for h in range(H):
-                cols = slice(h * NH, (h + 1) * NH)
-                picked = table[b][:].indirect(offsets[:, h * (NH // 16) : (h + 1) * (NH // 16)])
-                nc.vector.tensor_tensor(x[b][:, cols], picked, pos[b][:, cols], ALU.add)
-                if first:
-                    nc.tensor.matmul(shift[:, cols], mean_of_block[:], x[0][:, cols], start=True, stop=True)
-                nc.vector.tensor_tensor(d[:, b, cols], x[b][:, cols], shift[:, cols], ALU.subtract)
-                d2 = work.tile([P, NH], F32, name="d2")
-                nc.scalar.activation(d2[:], d[:, b, cols], ACT.Square)
-                nc.tensor.matmul(sum_d[h][:], mean_of_all[:], d[:, b, cols], start=first, stop=last)
-                nc.tensor.matmul(sum_d2[h][:], mean_of_all[:], d2[:], start=first, stop=last)
-            nc.sync.dma_start(out[b * P : (b + 1) * P, 0:N], x[b][:])
+            for t in range(NT):
+                tokens = slice(t * P, (t + 1) * P)
+                picked = table[b][:].indirect(offsets[:, t * (P // 16) : (t + 1) * (P // 16)])
+                nc.vector.tensor_tensor(x[:, b, tokens], picked, pos[b][:, tokens], ALU.add)
+                turned = psum.tile([P, P], F32, name="turned")
+                nc.tensor.transpose(turned[:], x[:, b, tokens], identity[:])
+                nc.vector.bn_stats(stats[:, t, b, :], turned[:])
+                nc.scalar.copy(x_turned[:, t, b * P : (b + 1) * P], turned[:])
+            nc.sync.dma_start(out[b * P : (b + 1) * P, 0:N], x[:, b, :])
 
-        mean_d = held.tile([P, N], F32, name="mean_d")
-        rstd = held.tile([P, N], F32, name="rstd")
-        rstd_psum = [psum.tile([P, NH], F32, name=f"rstd_psum{h}") for h in range(H)]
-        centred = held.tile([P, NB, N], F32, name="centred")
-
-        def statistics(h):
-            cols = slice(h * NH, (h + 1) * NH)
-            square_of_mean = work.tile([P, NH], F32, name="square_of_mean")
-            nc.scalar.activation(square_of_mean[:], sum_d[h][:], ACT.Square)
-            var = work.tile([P, NH], F32, name="var")
-            nc.vector.tensor_tensor(var[:], sum_d2[h][:], square_of_mean[:], ALU.subtract)
-            nc.scalar.activation(rstd[:, cols], var[:], ACT.Abs_reciprocal_sqrt, bias=eps[:])
-            nc.tensor.matmul(rstd_psum[h][:], identity[:], rstd[:, cols], start=True, stop=True)
-            nc.scalar.copy(mean_d[:, cols], sum_d[h][:])
-
-        def centre(h):
-            cols = slice(h * NH, (h + 1) * NH)
-            for b in range(NV):
-                nc.vector.tensor_tensor(centred[:, b, cols], d[:, b, cols], sum_d[h][:], ALU.subtract)
-            nc.gpsimd.tensor_tensor(
-                centred[:, NV:NB, cols], d[:, NV:NB, cols],
-                mean_d[:, cols].unsqueeze(1).to_broadcast([P, NB - NV, NH]), ALU.subtract,
+        mean_var = held.tile([P, NT, 2], F32, name="mean_var")
+        rstd = held.tile([P, NT], F32, name="rstd")
+        normed = held.tile([P, NT, C], F32, name="normed")
+        y = held.tile([P, NB, N], F32, name="y")
+        for t in range(NT):
+            tokens = slice(t * P, (t + 1) * P)
+            nc.vector.bn_aggr(mean_var[:, t, :], stats[:, t, :, :].rearrange("p b s -> p (b s)"))
+            nc.scalar.activation(rstd[:, t : t + 1], mean_var[:, t, 1:2], ACT.Abs_reciprocal_sqrt, bias=eps[:])
+            nc.vector.tensor_scalar(
+                normed[:, t, :], x_turned[:, t, :], mean_var[:, t, 0:1], rstd[:, t : t + 1],
+                ALU.subtract, ALU.mult,
             )
-
-        def finish(h):
-            cols = slice(h * NH, (h + 1) * NH)
             for b in range(NB):
-                normed = tail.tile([P, NH], F32, name="normed")
-                if b < NV:
-                    nc.vector.tensor_tensor(normed[:], centred[:, b, cols], rstd_psum[h][:], ALU.mult)
+                turned = psum.tile([P, P], F32, name="turned")
+                nc.tensor.transpose(turned[:], normed[:, t, b * P : (b + 1) * P], identity[:])
+                if b % 3 < 2:
+                    nc.scalar.activation(
+                        y[:, b, tokens], turned[:], ACT.Identity,
+                        bias=gain_bias[:, NB + b : NB + b + 1], scale=gain_bias[:, b : b + 1],
+                    )
                 else:
-                    nc.gpsimd.tensor_tensor(normed[:], centred[:, b, cols], rstd[:, cols], ALU.mult)
-                y = tail.tile([P, NH], F32, name="y")
-                nc.scalar.activation(
-                    y[:], normed[:], ACT.Identity,
-                    bias=gain_bias[:, NB + b : NB + b + 1], scale=gain_bias[:, b : b + 1],
-                )
-                nc.sync.dma_start(out[b * P : (b + 1) * P, N + h * NH : N + (h + 1) * NH], y[:])
-
-        statistics(0)
-        centre(0)
-        statistics(1)
-        finish(0)
-        centre(1)
-        finish(1)
+                    nc.vector.tensor_scalar(
+                        y[:, b, tokens], turned[:], gain_bias[:, b : b + 1], gain_bias[:, NB + b : NB + b + 1],
+                        ALU.mult, ALU.add,
+                    )
+                if t % 2 == 1:
+                    pair = slice((t - 1) * P, (t + 1) * P)
+                    nc.sync.dma_start(out[b * P : (b + 1) * P, N + (t - 1) * P : N + (t + 1) * P], y[:, b, pair])

@@ -18,7 +18,7 @@ def tile_trunk_model_kernel(tc, wte, wpe, gain, bias, offs, out):
     nc = tc.nc
     with (
         tc.tile_pool(name="held", bufs=1) as held,
-        tc.psum_pool(name="psum", bufs=8) as psum,
+        tc.psum_pool(name="psum", bufs=4) as psum,
     ):
         offsets = held.tile([P, N // 16], U16, name="offsets")
         nc.sync.dma_start(offsets[:], offs)
@@ -64,26 +64,28 @@ def tile_trunk_model_kernel(tc, wte, wpe, gain, bias, offs, out):
         normed = held.tile([P, NT, C], F32, name="normed")
         y = held.tile([P, NB, N], F32, name="y")
         for t in range(NT):
-            tokens = slice(t * P, (t + 1) * P)
             nc.vector.bn_aggr(mean_var[:, t, :], stats[:, t, :, :].rearrange("p b s -> p (b s)"))
             nc.scalar.activation(rstd[:, t : t + 1], mean_var[:, t, 1:2], ACT.Abs_reciprocal_sqrt, bias=eps[:])
-            nc.vector.tensor_scalar(
-                normed[:, t, :], x_turned[:, t, :], mean_var[:, t, 0:1], rstd[:, t : t + 1],
-                ALU.subtract, ALU.mult,
-            )
+        for h in range(NT // 2):
+            groups = (2 * h, 2 * h + 1)
+            half = slice(2 * h * P, (2 * h + 2) * P)
             for b in range(NB):
-                turned = psum.tile([P, P], F32, name="turned")
-                nc.tensor.transpose(turned[:], normed[:, t, b * P : (b + 1) * P], identity[:])
+                channels = slice(b * P, (b + 1) * P)
+                back = psum.tile([P, 2 * P], F32, name="back")
+                for t in groups:
+                    nc.vector.tensor_scalar(
+                        normed[:, t, channels], x_turned[:, t, channels], mean_var[:, t, 0:1], rstd[:, t : t + 1],
+                        ALU.subtract, ALU.mult,
+                    )
+                    nc.tensor.transpose(back[:, (t % 2) * P : (t % 2 + 1) * P], normed[:, t, channels], identity[:])
                 if b % 3 < 2:
                     nc.scalar.activation(
-                        y[:, b, tokens], turned[:], ACT.Identity,
+                        y[:, b, half], back[:], ACT.Identity,
                         bias=gain_bias[:, NB + b : NB + b + 1], scale=gain_bias[:, b : b + 1],
                     )
                 else:
                     nc.vector.tensor_scalar(
-                        y[:, b, tokens], turned[:], gain_bias[:, b : b + 1], gain_bias[:, NB + b : NB + b + 1],
+                        y[:, b, half], back[:], gain_bias[:, b : b + 1], gain_bias[:, NB + b : NB + b + 1],
                         ALU.mult, ALU.add,
                     )
-                if t % 2 == 1:
-                    pair = slice((t - 1) * P, (t + 1) * P)
-                    nc.sync.dma_start(out[b * P : (b + 1) * P, N + (t - 1) * P : N + (t + 1) * P], y[:, b, pair])
+                nc.sync.dma_start(out[channels, N + 2 * h * P : N + (2 * h + 2) * P], y[:, b, half])

@@ -18,7 +18,7 @@ def tile_trunk_model_kernel(tc, wte, wpe, gain, bias, offs, out):
     nc = tc.nc
     with (
         tc.tile_pool(name="held", bufs=1) as held,
-        tc.psum_pool(name="psum", bufs=4) as psum,
+        tc.psum_pool(name="psum", bufs=8) as psum,
     ):
         offsets = held.tile([P, N // 16], U16, name="offsets")
         nc.sync.dma_start(offsets[:], offs)
@@ -71,7 +71,7 @@ def tile_trunk_model_kernel(tc, wte, wpe, gain, bias, offs, out):
             half = slice(2 * h * P, (2 * h + 2) * P)
             for b in range(NB):
                 channels = slice(b * P, (b + 1) * P)
-                back = psum.tile([P, 2 * P], F32, name="back")
+                back = psum.tile([P, 2 * P], F32, name="back", tag="turned")
                 for t in groups:
                     nc.vector.tensor_scalar(
                         normed[:, t, channels], x_turned[:, t, channels], mean_var[:, t, 0:1], rstd[:, t : t + 1],

@@ -66,26 +66,25 @@ def tile_trunk_model_kernel(tc, wte, wpe, gain, bias, offs, out):
         for t in range(NT):
             nc.vector.bn_aggr(mean_var[:, t, :], stats[:, t, :, :].rearrange("p b s -> p (b s)"))
             nc.scalar.activation(rstd[:, t : t + 1], mean_var[:, t, 1:2], ACT.Abs_reciprocal_sqrt, bias=eps[:])
-        for h in range(NT // 2):
-            groups = (2 * h, 2 * h + 1)
-            half = slice(2 * h * P, (2 * h + 2) * P)
+        for groups in ((0,), (1, 2, 3)):
+            tokens = slice(groups[0] * P, (groups[-1] + 1) * P)
             for b in range(NB):
                 channels = slice(b * P, (b + 1) * P)
-                back = psum.tile([P, 2 * P], F32, name="back", tag="turned")
-                for t in groups:
+                back = psum.tile([P, len(groups) * P], F32, name="back", tag="turned")
+                for g, t in enumerate(groups):
                     nc.vector.tensor_scalar(
                         normed[:, t, channels], x_turned[:, t, channels], mean_var[:, t, 0:1], rstd[:, t : t + 1],
                         ALU.subtract, ALU.mult,
                     )
-                    nc.tensor.transpose(back[:, (t % 2) * P : (t % 2 + 1) * P], normed[:, t, channels], identity[:])
+                    nc.tensor.transpose(back[:, g * P : (g + 1) * P], normed[:, t, channels], identity[:])
                 if b % 3 < 2:
                     nc.scalar.activation(
-                        y[:, b, half], back[:], ACT.Identity,
+                        y[:, b, tokens], back[:], ACT.Identity,
                         bias=gain_bias[:, NB + b : NB + b + 1], scale=gain_bias[:, b : b + 1],
                     )
                 else:
                     nc.vector.tensor_scalar(
-                        y[:, b, half], back[:], gain_bias[:, b : b + 1], gain_bias[:, NB + b : NB + b + 1],
+                        y[:, b, tokens], back[:], gain_bias[:, b : b + 1], gain_bias[:, NB + b : NB + b + 1],
                         ALU.mult, ALU.add,
                     )
-                nc.sync.dma_start(out[channels, N + 2 * h * P : N + (2 * h + 2) * P], y[:, b, half])
+                nc.sync.dma_start(out[channels, N + groups[0] * P : N + (groups[-1] + 1) * P], y[:, b, tokens])

@@ -23,11 +23,17 @@ def tile_trunk_model_kernel(tc, wte, wpe, gain, bias, offs, out):
         offsets = held.tile([P, N // 16], U16, name="offsets")
         nc.sync.dma_start(offsets[:], offs)
         table = [held.tile([P, S], F32, name=f"table{b}") for b in range(NB)]
-        pos = [held.tile([P, N], F32, name=f"pos{b}") for b in range(NB)]
-        for b in range(NB):
+        last = NB - 1
+        pos = [held.tile([P, N], F32, name=f"pos{b}") for b in range(last)]
+        pos_last = [held.tile([P, N // 2], F32, name=f"pos_last{h}") for h in range(2)]
+        for b in range(last):
             rows = slice(b * P, (b + 1) * P)
             nc.sync.dma_start(pos[b][:], wpe[rows, :])
             nc.sync.dma_start(table[b][:], wte[rows, :])
+        rows = slice(last * P, C)
+        nc.sync.dma_start(pos_last[0][:], wpe[rows, 0 : N // 2])
+        nc.sync.dma_start(table[last][:], wte[rows, :])
+        nc.sync.dma_start(pos_last[1][:], wpe[rows, N // 2 : N])
 
         rows_gb = held.tile([P, P], F32, name="rows_gb")
         nc.vector.memset(rows_gb[:], 0.0)
@@ -48,25 +54,32 @@ def tile_trunk_model_kernel(tc, wte, wpe, gain, bias, offs, out):
         x = held.tile([P, NB, N], F32, name="x")
         x_turned = held.tile([P, NT, C], F32, name="x_turned")
         stats = held.tile([P, NT, NB, STATS], F32, name="stats")
-        for b in range(NB):
-            for t in range(NT):
-                tokens = slice(t * P, (t + 1) * P)
-                picked = table[b][:].indirect(offsets[:, t * (P // 16) : (t + 1) * (P // 16)])
-                nc.vector.tensor_tensor(x[:, b, tokens], picked, pos[b][:, tokens], ALU.add)
-                turned = psum.tile([P, P], F32, name="turned")
-                nc.tensor.transpose(turned[:], x[:, b, tokens], identity[:])
-                nc.vector.bn_stats(stats[:, t, b, :], turned[:])
-                nc.scalar.copy(x_turned[:, t, b * P : (b + 1) * P], turned[:])
-            nc.sync.dma_start(out[b * P : (b + 1) * P, 0:N], x[:, b, :])
-
         mean_var = held.tile([P, NT, 2], F32, name="mean_var")
         rstd = held.tile([P, NT], F32, name="rstd")
         normed = held.tile([P, NT, C], F32, name="normed")
         y = held.tile([P, NB, N], F32, name="y")
-        for t in range(NT):
+
+        def look_up(b, t):
+            tokens = slice(t * P, (t + 1) * P)
+            picked = table[b][:].indirect(offsets[:, t * (P // 16) : (t + 1) * (P // 16)])
+            if b < last:
+                positions = pos[b][:, tokens]
+            else:
+                positions = pos_last[t // 2][:, (t % 2) * P : (t % 2 + 1) * P]
+            nc.vector.tensor_tensor(x[:, b, tokens], picked, positions, ALU.add)
+            turned = psum.tile([P, P], F32, name="turned")
+            nc.tensor.transpose(turned[:], x[:, b, tokens], identity[:])
+            nc.vector.bn_stats(stats[:, t, b, :], turned[:])
+            nc.scalar.copy(x_turned[:, t, b * P : (b + 1) * P], turned[:])
+
+        def store_x(b):
+            nc.sync.dma_start(out[b * P : (b + 1) * P, 0:N], x[:, b, :])
+
+        def statistics(t):
             nc.vector.bn_aggr(mean_var[:, t, :], stats[:, t, :, :].rearrange("p b s -> p (b s)"))
             nc.scalar.activation(rstd[:, t : t + 1], mean_var[:, t, 1:2], ACT.Abs_reciprocal_sqrt, bias=eps[:])
-        for groups in ((0,), (1, 2, 3)):
+
+        def way_back(groups):
             tokens = slice(groups[0] * P, (groups[-1] + 1) * P)
             for b in range(NB):
                 channels = slice(b * P, (b + 1) * P)
@@ -88,3 +101,12 @@ def tile_trunk_model_kernel(tc, wte, wpe, gain, bias, offs, out):
                         ALU.mult, ALU.add,
                     )
                 nc.sync.dma_start(out[channels, N + groups[0] * P : N + (groups[-1] + 1) * P], y[:, b, tokens])
+
+        for b in range(NB):
+            for t in range(NT):
+                look_up(b, t)
+            store_x(b)
+        for t in range(NT):
+            statistics(t)
+        way_back((0,))
+        way_back((1, 2, 3))

@@ -24,12 +24,16 @@ def tile_trunk_model_kernel(tc, wte, wpe, gain, bias, offs, out):
         nc.sync.dma_start(offsets[:], offs)
         table = [held.tile([P, S], F32, name=f"table{b}") for b in range(NB)]
         last = NB - 1
-        pos = [held.tile([P, N], F32, name=f"pos{b}") for b in range(last)]
+        pos_pair = [held.tile([P, 2, N], F32, name=f"pos_pair{h}") for h in range(2)]
+        pos_fifth = held.tile([P, N], F32, name="pos_fifth")
         pos_last = [held.tile([P, N // 2], F32, name=f"pos_last{h}") for h in range(2)]
         for b in range(last):
-            rows = slice(b * P, (b + 1) * P)
-            nc.sync.dma_start(pos[b][:], wpe[rows, :])
-            nc.sync.dma_start(table[b][:], wte[rows, :])
+            if b < 4 and b % 2 == 0:
+                both = wpe[b * P : (b + 2) * P, :].rearrange("(b p) j -> p b j", p=P)
+                nc.sync.dma_start(pos_pair[b // 2][:], both)
+            if b == 4:
+                nc.sync.dma_start(pos_fifth[:], wpe[b * P : (b + 1) * P, :])
+            nc.sync.dma_start(table[b][:], wte[b * P : (b + 1) * P, :])
         rows = slice(last * P, C)
         nc.sync.dma_start(pos_last[0][:], wpe[rows, 0 : N // 2])
         nc.sync.dma_start(table[last][:], wte[rows, :])
@@ -62,8 +66,10 @@ def tile_trunk_model_kernel(tc, wte, wpe, gain, bias, offs, out):
         def look_up(b, t):
             tokens = slice(t * P, (t + 1) * P)
             picked = table[b][:].indirect(offsets[:, t * (P // 16) : (t + 1) * (P // 16)])
-            if b < last:
-                positions = pos[b][:, tokens]
+            if b < 4:
+                positions = pos_pair[b // 2][:, b % 2, tokens]
+            elif b == 4:
+                positions = pos_fifth[:, tokens]
             else:
                 positions = pos_last[t // 2][:, (t % 2) * P : (t % 2 + 1) * P]
             nc.vector.tensor_tensor(x[:, b, tokens], picked, positions, ALU.add)

@@ -45,10 +45,7 @@ def tile_trunk_model_kernel(tc, wte, wpe, gain, bias, offs, out):
         nc.scalar.dma_start(rows_gb[NB : 2 * NB, :], bias.rearrange("(b p) o -> b (p o)", p=P))
         identity = held.tile([P, P], F32, name="identity")
         masks.make_identity(nc, identity[:])
-        turned_gb = psum.tile([P, P], F32, name="turned_gb", tag="turned")
-        nc.tensor.transpose(turned_gb[:], rows_gb[:], identity[:])
         gain_bias = held.tile([P, 2 * NB], F32, name="gain_bias")
-        nc.vector.tensor_copy(gain_bias[:], turned_gb[:, 0 : 2 * NB])
 
         eps = held.tile([P, 1], F32, name="eps")
         nc.vector.memset(eps[:], EPS)
@@ -112,6 +109,10 @@ def tile_trunk_model_kernel(tc, wte, wpe, gain, bias, offs, out):
             for t in range(NT):
                 look_up(b, t)
             store_x(b)
+            if b == NB // 2:
+                turned_gb = psum.tile([P, P], F32, name="turned_gb", tag="turned")
+                nc.tensor.transpose(turned_gb[:], rows_gb[:], identity[:])
+                nc.vector.tensor_copy(gain_bias[:], turned_gb[:, 0 : 2 * NB])
         for t in range(NT):
             statistics(t)
         way_back((0,))

@@ -11,6 +11,7 @@ C, S, N = 768, 2048, 512
 NB = C // P
 NT = N // P
 STATS = 6
+EARLY = 3
 EPS = 1e-5
 
 
@@ -24,15 +25,14 @@ def tile_trunk_model_kernel(tc, wte, wpe, gain, bias, offs, out):
         nc.sync.dma_start(offsets[:], offs)
         table = [held.tile([P, S], F32, name=f"table{b}") for b in range(NB)]
         last = NB - 1
-        pos_pair = [held.tile([P, 2, N], F32, name=f"pos_pair{h}") for h in range(2)]
-        pos_fifth = held.tile([P, N], F32, name="pos_fifth")
+        pos_early = held.tile([P, EARLY, N], F32, name="pos_early")
+        pos_late = held.tile([P, last - EARLY, N], F32, name="pos_late")
         pos_last = [held.tile([P, N // 2], F32, name=f"pos_last{h}") for h in range(2)]
-        for b in range(last):
-            if b < 4 and b % 2 == 0:
-                both = wpe[b * P : (b + 2) * P, :].rearrange("(b p) j -> p b j", p=P)
-                nc.sync.dma_start(pos_pair[b // 2][:], both)
-            if b == 4:
-                nc.sync.dma_start(pos_fifth[:], wpe[b * P : (b + 1) * P, :])
+        nc.sync.dma_start(pos_early[:], wpe[0 : EARLY * P, :].rearrange("(b p) j -> p b j", p=P))
+        for b in range(EARLY):
+            nc.sync.dma_start(table[b][:], wte[b * P : (b + 1) * P, :])
+        nc.sync.dma_start(pos_late[:], wpe[EARLY * P : last * P, :].rearrange("(b p) j -> p b j", p=P))
+        for b in range(EARLY, last):
             nc.sync.dma_start(table[b][:], wte[b * P : (b + 1) * P, :])
         rows = slice(last * P, C)
         nc.sync.dma_start(pos_last[0][:], wpe[rows, 0 : N // 2])
@@ -54,7 +54,7 @@ def tile_trunk_model_kernel(tc, wte, wpe, gain, bias, offs, out):
 
         x = held.tile([P, NB, N], F32, name="x")
         x_turned = held.tile([P, NT, C], F32, name="x_turned")
-        stats = held.tile([P, NT, NB, STATS], F32, name="stats")
+        stats = held.tile([P, NT, 1 + NB - EARLY, STATS], F32, name="stats")
         mean_var = held.tile([P, NT, 2], F32, name="mean_var")
         rstd = held.tile([P, NT], F32, name="rstd")
         normed = held.tile([P, NT, C], F32, name="normed")
@@ -63,16 +63,17 @@ def tile_trunk_model_kernel(tc, wte, wpe, gain, bias, offs, out):
         def look_up(b, t):
             tokens = slice(t * P, (t + 1) * P)
             picked = table[b][:].indirect(offsets[:, t * (P // 16) : (t + 1) * (P // 16)])
-            if b < 4:
-                positions = pos_pair[b // 2][:, b % 2, tokens]
-            elif b == 4:
-                positions = pos_fifth[:, tokens]
+            if b < EARLY:
+                positions = pos_early[:, b, tokens]
+            elif b < last:
+                positions = pos_late[:, b - EARLY, tokens]
             else:
                 positions = pos_last[t // 2][:, (t % 2) * P : (t % 2 + 1) * P]
             nc.vector.tensor_tensor(x[:, b, tokens], picked, positions, ALU.add)
             turned = psum.tile([P, P], F32, name="turned")
             nc.tensor.transpose(turned[:], x[:, b, tokens], identity[:])
-            nc.vector.bn_stats(stats[:, t, b, :], turned[:])
+            if b >= EARLY:
+                nc.vector.bn_stats(stats[:, t, 1 + b - EARLY, :], turned[:])
             nc.scalar.copy(x_turned[:, t, b * P : (b + 1) * P], turned[:])
 
         def store_x(b):
@@ -109,6 +110,9 @@ def tile_trunk_model_kernel(tc, wte, wpe, gain, bias, offs, out):
             for t in range(NT):
                 look_up(b, t)
             store_x(b)
+            if b == EARLY - 1:
+                for t in range(NT):
+                    nc.vector.bn_stats(stats[:, t, 0, :], x_turned[:, t, 0 : EARLY * P])
             if b == NB // 2:
                 turned_gb = psum.tile([P, P], F32, name="turned_gb", tag="turned")
                 nc.tensor.transpose(turned_gb[:], rows_gb[:], identity[:])

import concourse.masks as masks
import concourse.mybir as mybir

F32 = mybir.dt.float32
U16 = mybir.dt.uint16
ALU = mybir.AluOpType
ACT = mybir.ActivationFunctionType

P = 128
C, S, N = 768, 2048, 512
NB = C // P
NT = N // P
STATS = 6
EARLY = 3
EPS = 1e-5


def tile_trunk_model_kernel(tc, wte, wpe, gain, bias, offs, out):
    nc = tc.nc
    with (
        tc.tile_pool(name="held", bufs=1) as held,
        tc.psum_pool(name="psum", bufs=8) as psum,
    ):
        offsets = held.tile([P, N // 16], U16, name="offsets")
        nc.sync.dma_start(offsets[:], offs)
        table = [held.tile([P, S], F32, name=f"table{b}") for b in range(NB)]
        last = NB - 1
        pos_early = held.tile([P, EARLY, N], F32, name="pos_early")
        pos_late = held.tile([P, last - EARLY, N], F32, name="pos_late")
        pos_last = [held.tile([P, N // 2], F32, name=f"pos_last{h}") for h in range(2)]
        nc.sync.dma_start(pos_early[:], wpe[0 : EARLY * P, :].rearrange("(b p) j -> p b j", p=P))
        for b in range(EARLY):
            nc.sync.dma_start(table[b][:], wte[b * P : (b + 1) * P, :])
        nc.sync.dma_start(pos_late[:], wpe[EARLY * P : last * P, :].rearrange("(b p) j -> p b j", p=P))
        for b in range(EARLY, last):
            nc.sync.dma_start(table[b][:], wte[b * P : (b + 1) * P, :])
        rows = slice(last * P, C)
        nc.sync.dma_start(pos_last[0][:], wpe[rows, 0 : N // 2])
        nc.sync.dma_start(table[last][:], wte[rows, :])
        nc.sync.dma_start(pos_last[1][:], wpe[rows, N // 2 : N])

        rows_gb = held.tile([P, P], F32, name="rows_gb")
        nc.vector.memset(rows_gb[:], 0.0)
        nc.scalar.dma_start(rows_gb[0:NB, :], gain.rearrange("(b p) o -> b (p o)", p=P))
        nc.scalar.dma_start(rows_gb[NB : 2 * NB, :], bias.rearrange("(b p) o -> b (p o)", p=P))
        identity = held.tile([P, P], F32, name="identity")
        masks.make_identity(nc, identity[:])
        gain_bias = held.tile([P, 2 * NB], F32, name="gain_bias")

        eps = held.tile([P, 1], F32, name="eps")
        nc.vector.memset(eps[:], EPS)
        warm = held.tile([P, 1], F32, name="warm")
        nc.scalar.activation(warm[:], eps[:], ACT.Abs_reciprocal_sqrt)

        x = held.tile([P, NB, N], F32, name="x")
        x_turned = held.tile([P, NT, C], F32, name="x_turned")
        stats = held.tile([P, NT, 1 + NB - EARLY, STATS], F32, name="stats")
        mean_var = held.tile([P, NT, 2], F32, name="mean_var")
        rstd = held.tile([P, NT], F32, name="rstd")
        normed = held.tile([P, NT, C], F32, name="normed")
        y = held.tile([P, NB, N], F32, name="y")

        def look_up(b, t):
            tokens = slice(t * P, (t + 1) * P)
            picked = table[b][:].indirect(offsets[:, t * (P // 16) : (t + 1) * (P // 16)])
            if b < EARLY:
                positions = pos_early[:, b, tokens]
            elif b < last:
                positions = pos_late[:, b - EARLY, tokens]
            else:
                positions = pos_last[t // 2][:, (t % 2) * P : (t % 2 + 1) * P]
            nc.vector.tensor_tensor(x[:, b, tokens], picked, positions, ALU.add)
            turned = psum.tile([P, P], F32, name="turned")
            nc.tensor.transpose(turned[:], x[:, b, tokens], identity[:])
            if b >= EARLY:
                nc.vector.bn_stats(stats[:, t, 1 + b - EARLY, :], turned[:])
            nc.scalar.copy(x_turned[:, t, b * P : (b + 1) * P], turned[:])

        def store_x(b):
            nc.sync.dma_start(out[b * P : (b + 1) * P, 0:N], x[:, b, :])

        def statistics(t):
            nc.vector.bn_aggr(mean_var[:, t, :], stats[:, t, :, :].rearrange("p b s -> p (b s)"))
            nc.scalar.activation(rstd[:, t : t + 1], mean_var[:, t, 1:2], ACT.Abs_reciprocal_sqrt, bias=eps[:])

        def way_back(groups):
            tokens = slice(groups[0] * P, (groups[-1] + 1) * P)
            for b in range(NB):
                channels = slice(b * P, (b + 1) * P)
                back = psum.tile([P, len(groups) * P], F32, name="back", tag="turned")
                for g, t in enumerate(groups):
                    nc.vector.tensor_scalar(
                        normed[:, t, channels], x_turned[:, t, channels], mean_var[:, t, 0:1], rstd[:, t : t + 1],
                        ALU.subtract, ALU.mult,
                    )
                    nc.tensor.transpose(back[:, g * P : (g + 1) * P], normed[:, t, channels], identity[:])
                if b % 3 < 2:
                    nc.scalar.activation(
                        y[:, b, tokens], back[:], ACT.Identity,
                        bias=gain_bias[:, NB + b : NB + b + 1], scale=gain_bias[:, b : b + 1],
                    )
                else:
                    nc.vector.tensor_scalar(
                        y[:, b, tokens], back[:], gain_bias[:, b : b + 1], gain_bias[:, NB + b : NB + b + 1],
                        ALU.mult, ALU.add,
                    )
                nc.sync.dma_start(out[channels, N + groups[0] * P : N + (groups[-1] + 1) * P], y[:, b, tokens])

        for b in range(NB):
            for t in range(NT):
                look_up(b, t)
            store_x(b)
            if b == EARLY - 1:
                for t in range(NT):
                    nc.vector.bn_stats(stats[:, t, 0, :], x_turned[:, t, 0 : EARLY * P])
            if b == NB // 2:
                turned_gb = psum.tile([P, P], F32, name="turned_gb", tag="turned")
                nc.tensor.transpose(turned_gb[:], rows_gb[:], identity[:])
                nc.vector.tensor_copy(gain_bias[:], turned_gb[:, 0 : 2 * NB])
        for t in range(NT):
            statistics(t)
        way_back((0,))
        way_back((1, 2, 3))
